import numpy as np
import ml_dtypes


def mxq(x, axis, fmt="e4m3"):
    dtype, down = {"e4m3": (ml_dtypes.float8_e4m3fn, 7), "e5m2": (ml_dtypes.float8_e5m2, 14)}[fmt]
    v = np.moveaxis(np.asarray(x, np.float32).astype(ml_dtypes.bfloat16).astype(np.float64), axis, -1)
    blocks = v.reshape(v.shape[:-1] + (-1, 32))
    amax = np.abs(blocks).max(-1, keepdims=True)
    byte = np.maximum(np.where(amax > 0, np.frexp(amax)[1] - 1 + 127, 0) - down, 1)
    scale = np.exp2(byte - 127.0)
    codes = (blocks / scale).astype(np.float32).astype(dtype).astype(np.float64)
    return np.moveaxis((codes * scale).reshape(v.shape), -1, axis)


WIDE = False


def mx_kscale(k):
    if not WIDE:
        return np.ones(k)
    levels = np.array([10, -10, 5, -5, 0])
    if k % 512:
        return np.exp2(np.random.permutation(np.resize(levels, k // 32))).repeat(32)
    a = np.empty((k // 512, 16))
    for p in range(k // 512):
        a[p, :8] = np.random.permutation(np.resize(levels, 8))
        for g in range(8):
            far = levels[np.abs(levels - a[p, g]) >= 10]
            a[p, g + 8] = far[np.random.randint(len(far))]
    return np.exp2(a.ravel()).repeat(32)


BF16 = ml_dtypes.bfloat16


def bf(x):
    return np.asarray(x, np.float32).astype(BF16)


def f64(x):
    return np.asarray(x).astype(np.float64)


B, DIM, E, HID = 1024, 1024, 1024, 2048
EPS = 1e-5


def layer_norm(y, g, b):
    m = y.mean(-1, keepdims=True)
    v = ((y - m) ** 2).mean(-1, keepdims=True)
    return (y - m) / np.sqrt(v + EPS) * g + b


def setup_inputs():
    s, t = mx_kscale(DIM), mx_kscale(E)
    r = np.random.standard_normal
    return {'feat': bf(r((B, DIM))),
            'own_self': bf(r((B, DIM))),
            'other_self': bf(r((B, DIM)) * s),
            'Wv': bf(r((E, DIM)) / np.sqrt(DIM) / s[None, :] * t[:, None]),
            'bv': bf(r(E) * 0.2 * t),
            'Wo': bf(r((DIM, E)) / np.sqrt(E) / t[None, :]),
            'bo': bf(r(DIM) * 0.2),
            'g': bf(1.0 + 0.1 * r(DIM)),
            'be': bf(0.1 * r(DIM))}


def reference(feat, own_self, other_self, Wv, bv, Wo, bo, g, be):
    val = (mxq(f64(other_self), 1, 'e4m3') @ mxq(f64(Wv), 1, 'e4m3').T) + f64(bv)
    cross = (mxq(val, 1, 'e4m3') @ mxq(f64(Wo), 1, 'e4m3').T) + f64(bo)
    return layer_norm(f64(feat) + (f64(own_self) + cross) * 0.5, f64(g), f64(be))

@@ -1,0 +1,334 @@
+from contextlib import ExitStack
+
+import concourse.mybir as mybir
+from concourse.masks import make_identity
+
+BF16 = mybir.dt.bfloat16
+F32 = mybir.dt.float32
+I32 = mybir.dt.int32
+U32 = mybir.dt.uint32
+U8 = mybir.dt.uint8
+FP8X4 = mybir.dt.float8_e4m3fn_x4
+ACT = mybir.ActivationFunctionType
+ALU = mybir.AluOpType
+
+P = 128
+SIZE = 1024
+PACK = 4
+PASSES = SIZE // (P * PACK)
+TILES = SIZE // P
+PAIRS = TILES // 2
+HALF = 512
+HALF_TILES = HALF // P
+BANK_BLOCKS = HALF // P
+VECTOR_TURN = 4
+EPS = 1e-5
+
+FLOPS = 2 * 2 * SIZE * SIZE * SIZE
+
+
+def tile_efficientfusionlayer_pb_kernel(
+    tc, feat, own_self, other_self, Wv, bv, Wo, bo, g, be, out
+):
+    nc = tc.nc
+
+    def batch_pairs(matrix):
+        view = matrix.rearrange("(p j e) d -> p j e d", j=PAIRS, e=2)
+        return [view[:, j] for j in range(PAIRS)]
+
+    x_view, feat_view, own_view = [batch_pairs(m) for m in (other_self, feat, own_self)]
+    out_view = out.rearrange("(p t) d -> p t d", t=TILES)
+    wv_rows = Wv.rearrange("(c p t) d -> p c t d", c=PASSES, t=PACK)
+    wv_view = [wv_rows[:, j // 2, 2 * (j % 2) : 2 * (j % 2) + 2] for j in range(PAIRS)]
+    bv_view = bv.rearrange("(c p t) -> p c t", c=PASSES, t=PACK)
+    wo_rows = Wo.rearrange("(j e p) v -> p j e v", j=PAIRS, e=2)
+    wo_view = [wo_rows[:, j] for j in range(PAIRS)]
+    bo_view = bo.rearrange("(i p) -> p i", p=P)
+
+    with ExitStack() as pools:
+        const = pools.enter_context(tc.tile_pool(name="const", bufs=1))
+        keep = pools.enter_context(tc.tile_pool(name="keep", bufs=1))
+        weight_rows = pools.enter_context(tc.tile_pool(name="weight_rows", bufs=6))
+        stage_one = pools.enter_context(tc.tile_pool(name="stage_one", bufs=4))
+        stage_half = pools.enter_context(tc.tile_pool(name="stage_half", bufs=1))
+        work = pools.enter_context(tc.tile_pool(name="work", bufs=2))
+        normed = pools.enter_context(tc.tile_pool(name="normed", bufs=3))
+        small = pools.enter_context(tc.tile_pool(name="small", bufs=3))
+        psum_chain = pools.enter_context(tc.psum_pool(name="psum_chain", bufs=4))
+        psum_back = pools.enter_context(tc.psum_pool(name="psum_back", bufs=4))
+
+        def load_pair(pool, view, j, name):
+            rows = pool.tile([P, 2, SIZE], BF16, tag=name)
+            nc.sync.dma_start(out=rows[:], in_=view[j])
+            return rows
+
+        def empty_bank(turn, out_ap, bank, scale, bias_col):
+            if turn % VECTOR_TURN == VECTOR_TURN - 1:
+                nc.vector.tensor_scalar(
+                    out=out_ap, in0=bank, scalar1=scale, scalar2=bias_col, op0=ALU.mult, op1=ALU.add
+                )
+            else:
+                nc.scalar.activation(
+                    out=out_ap, in_=bank, func=ACT.Identity, bias=bias_col, scale=scale
+                )
+
+        norm_rows = const.tile([P, 2, SIZE], BF16)
+        nc.vector.memset(norm_rows[:].bitcast(I32), 0)
+        nc.sync.dma_start(out=norm_rows[0:1, 0, :], in_=g.unsqueeze(0))
+        nc.sync.dma_start(out=norm_rows[0:1, 1, :], in_=be.unsqueeze(0))
+        bv_raw = const.tile([P, TILES], BF16)
+        nc.sync.dma_start(out=bv_raw[:].rearrange("p (c t) -> p c t", t=PACK), in_=bv_view)
+        bo_raw = const.tile([P, TILES], BF16)
+        with nc.allow_non_contiguous_dma(reason="1024 bias values, one to a partition"):
+            nc.sync.dma_start(out=bo_raw[:], in_=bo_view)
+        x_rows = [load_pair(weight_rows, x_view, k, "rows") for k in range(2)]
+
+        ident = const.tile([P, P], F32)
+        make_identity(nc, ident[:])
+        ident_bf = const.tile([P, P], BF16)
+        make_identity(nc, ident_bf[:])
+        ones_bf = const.tile([P, P], BF16)
+        nc.vector.memset(ones_bf[:], 1.0)
+        eps_col = const.tile([P, 1], F32)
+        nc.vector.memset(eps_col[:], EPS)
+        warm = const.tile([P, 1], F32)
+        nc.scalar.activation(out=warm[:], in_=eps_col[:], func=ACT.Sqrt)
+
+
+        def convert_biases():
+            nc.vector.tensor_copy(out=bv_col[:], in_=bv_raw[:])
+            nc.vector.tensor_scalar(
+                out=half_bo_col[:], in0=bo_raw[:], scalar1=0.5, scalar2=None, op0=ALU.mult
+            )
+
+        def spread_norm_rows():
+            for v in range(2):
+                for k in range(2):
+                    cols = slice(k * HALF, (k + 1) * HALF)
+                    spread = psum_back.tile([P, HALF], F32, tag="back")
+                    nc.tensor.matmul(
+                        out=spread[:], lhsT=ones_bf[:], rhs=norm_rows[:, v, cols], start=True, stop=True
+                    )
+                    nc.vector.tensor_copy(out=norm_all[:, v, cols], in_=spread[:])
+
+        bv_col = const.tile([P, TILES], F32)
+        half_bo_col = const.tile([P, TILES], F32)
+        norm_all = const.tile([P, 2, SIZE], BF16)
+        g_all = norm_all[:, 0, :]
+        be_all = norm_all[:, 1, :]
+
+        def transpose_rows(stage, row_tiles, first_turn, vector_helps):
+            n_rows = P * len(row_tiles)
+            grouped = stage.tile([P, PASSES, n_rows, PACK], BF16, tag="grouped", align_bytes=64)
+            grouped_words = grouped[:].bitcast(F32)
+            for n, rows in enumerate(row_tiles):
+                words = rows.bitcast(F32)
+                turned = psum_chain.tile([P, PASSES, 2, P], F32, tag="chain")
+                for c in range(PASSES):
+                    for u in range(2):
+                        every_second = words[:, 2 * P * c + u : 2 * P * (c + 1) : 2]
+                        nc.tensor.transpose(turned[:, c, u, :], every_second, ident[:])
+                copy_out = grouped_words[:, :, n * P : (n + 1) * P, :]
+                copy_in = turned[:].rearrange("p c u r -> p c r u")
+                if vector_helps and (first_turn + n) % VECTOR_TURN == VECTOR_TURN - 1:
+                    nc.vector.tensor_copy(out=copy_out, in_=copy_in)
+                else:
+                    nc.scalar.copy(out=copy_out, in_=copy_in)
+            return grouped
+
+        def quantise(grouped, name):
+            n_rows = grouped.shape[2]
+            codes = keep.tile([P, PASSES, n_rows], U32, name=name + "_codes", align_bytes=64)
+            scales = keep.tile([P, PASSES, n_rows], U8, name=name + "_scales", align_bytes=64)
+            nc.vector.quantize_mx(
+                out=codes[:].rearrange("p c r -> p (c r)").bitcast(FP8X4),
+                scales=scales[:].rearrange("p c r -> p (c r)"),
+                in_=grouped[:].rearrange("p c r t -> p (c r t)"),
+            )
+            return codes, scales
+
+        def mx_product(acc, stationary, moving):
+            for c in range(PASSES):
+                nc.tensor.matmul_mx(
+                    out=acc,
+                    lhsT=stationary[0][:, c, :].bitcast(FP8X4),
+                    lhsT_scale=stationary[1][:, c, :],
+                    rhs=moving[0][:, c, :].bitcast(FP8X4),
+                    rhs_scale=moving[1][:, c, :],
+                    start=(c == 0),
+                    stop=(c == PASSES - 1),
+                )
+
+        def quantise_weight(view, name, pairs, quantised, vector_helps):
+            waiting = None
+            for j in pairs:
+                rows = load_pair(weight_rows, view, j, "rows")
+                for e in range(2):
+                    grouped = transpose_rows(stage_one, [rows[:, e, :]], 2 * j + e, vector_helps)
+                    if waiting is not None:
+                        quantised.append(quantise(waiting, "%s%d" % (name, len(quantised))))
+                    waiting = grouped
+            quantised.append(quantise(waiting, "%s%d" % (name, len(quantised))))
+
+        def value_products(x_q, c, vector_helps):
+            planes = work.tile([P, PACK, HALF], BF16, tag="planes")
+            for t in range(PACK):
+                acc = psum_chain.tile([P, HALF], F32, tag="chain")
+                mx_product(acc[:], wv_q[PACK * c + t], x_q)
+                bias_col = bv_col[:, PACK * c + t : PACK * c + t + 1]
+                empty_bank(t if vector_helps else 0, planes[:, t, :], acc[:], 1.0, bias_col)
+            return planes
+
+        def value_quantise(planes, val_q, c):
+            grouped = work.tile([P, HALF, PACK], BF16, tag="val_grouped", align_bytes=64)
+            nc.vector.tensor_copy(
+                out=grouped[:].rearrange("p (n i) t -> p n t i", i=4),
+                in_=planes[:].rearrange("p t (n i) -> p n t i", i=4),
+            )
+            nc.vector.quantize_mx(
+                out=val_q[0][:, c, :].bitcast(FP8X4),
+                scales=val_q[1][:, c, :],
+                in_=grouped[:].rearrange("p n t -> p (n t)"),
+            )
+
+        def new_val(h):
+            codes = keep.tile([P, PASSES, HALF], U32, name="val%d_codes" % h, align_bytes=64)
+            scales = keep.tile([P, PASSES, HALF], U8, name="val%d_scales" % h, align_bytes=64)
+            return codes, scales
+
+        def cross_products(val_q, cross_t, tiles, vector_helps):
+            for i in tiles:
+                acc = psum_chain.tile([P, HALF], F32, tag="chain")
+                mx_product(acc[:], wo_q[i], val_q)
+                empty_bank(
+                    i if vector_helps else 0, cross_t[:, i, :], acc[:], 0.5, half_bo_col[:, i : i + 1]
+                )
+
+        def gather(t, cross_t):
+            first = (t % HALF_TILES) * P
+            feat_rows = resid[t // 2][0][:, t % 2, :]
+            banks = []
+            for k in range(2):
+                back = psum_back.tile([P, BANK_BLOCKS, P], F32, tag="back")
+                nc.tensor.matmul(
+                    out=back[:].rearrange("p n r -> p (n r)"),
+                    lhsT=ident_bf[:],
+                    rhs=feat_rows[:, k * HALF : (k + 1) * HALF],
+                    start=True,
+                    stop=False,
+                )
+                for n in range(BANK_BLOCKS):
+                    nc.tensor.matmul(
+                        out=back[:, n, :],
+                        lhsT=cross_t[:, BANK_BLOCKS * k + n, first : first + P],
+                        rhs=ident[:],
+                        is_transpose=True,
+                        start=False,
+                        stop=(n == BANK_BLOCKS - 1),
+                    )
+                banks.append(back)
+            return banks
+
+        def centre(t, banks):
+            own_rows = resid[t // 2][1][:, t % 2, :]
+            y = work.tile([P, SIZE], F32, tag="y")
+            sums = small.tile([P, 2], F32, tag="sums")
+            for k in range(2):
+                cols = slice(k * HALF, (k + 1) * HALF)
+                nc.vector.scalar_tensor_tensor(
+                    out=y[:, cols],
+                    in0=own_rows[:, cols],
+                    scalar=0.5,
+                    in1=banks[k][:].rearrange("p n r -> p (n r)"),
+                    op0=ALU.mult,
+                    op1=ALU.add,
+                    accum_out=sums[:, k : k + 1],
+                )
+            neg_mean = small.tile([P, 1], F32, tag="neg_mean")
+            nc.vector.tensor_scalar(
+                out=neg_mean[:],
+                in0=sums[:, 0:1],
+                scalar1=sums[:, 1:2],
+                scalar2=-1.0 / SIZE,
+                op0=ALU.add,
+                op1=ALU.mult,
+            )
+            squares = work.tile([P, SIZE], BF16, tag="squares")
+            sum_sq = small.tile([P, 1], F32, tag="sum_sq")
+            nc.scalar.activation(
+                out=squares[:],
+                in_=y[:],
+                func=ACT.Square,
+                bias=neg_mean[:],
+                scale=1.0,
+                accum_out=sum_sq[:],
+            )
+            std = small.tile([P, 1], F32, tag="std")
+            nc.scalar.activation(
+                out=std[:], in_=sum_sq[:], func=ACT.Sqrt, bias=eps_col[:], scale=1.0 / SIZE
+            )
+            result = normed.tile([P, SIZE], F32, tag="result")
+            nc.vector.scalar_tensor_tensor(
+                out=result[:], in0=y[:], scalar=neg_mean[:], in1=g_all, op0=ALU.add, op1=ALU.mult
+            )
+            return result, std
+
+        def finish(t, centred):
+            result, std = centred
+            rstd = small.tile([P, 1], F32, tag="rstd")
+            nc.vector.reciprocal(out=rstd[:], in_=std[:])
+            nc.vector.scalar_tensor_tensor(
+                out=result[:], in0=result[:], scalar=rstd[:], in1=be_all, op0=ALU.mult, op1=ALU.add
+            )
+            nc.sync.dma_start(out=out_view[:, t, :], in_=result[:])
+
+        def load_resid(j):
+            return load_pair(keep, feat_view, j, "feat%d" % j), load_pair(keep, own_view, j, "own%d" % j)
+
+        def halves(rows_list):
+            return [rows[:, e, :] for rows in rows_list for e in range(2)]
+
+        x_grouped = transpose_rows(stage_half, halves(x_rows), 0, True)
+        x_q0 = quantise(x_grouped, "x0")
+        convert_biases()
+        wv_q = []
+        quantise_weight(wv_view, "wv", range(0, 2), wv_q, True)
+        val_q0 = new_val(0)
+        wo_q = []
+        planes0 = value_products(x_q0, 0, True)
+        quantise_weight(wv_view, "wv", range(2, 4), wv_q, True)
+        value_quantise(planes0, val_q0, 0)
+        planes1 = value_products(x_q0, 1, True)
+        quantise_weight(wo_view, "wo", range(0, 1), wo_q, False)
+        value_quantise(planes1, val_q0, 1)
+        quantise_weight(wo_view, "wo", range(1, 4), wo_q, False)
+        x_rows = [load_pair(weight_rows, x_view, 2 + k, "rows") for k in range(2)]
+        resid = [load_resid(j) for j in range(PAIRS)]
+        spread_norm_rows()
+        cross_t0 = keep.tile([P, TILES, HALF], F32, name="cross_t0")
+        cross_products(val_q0, cross_t0, range(TILES), True)
+
+        val_q1 = new_val(1)
+        cross_t1 = keep.tile([P, TILES, HALF], F32, name="cross_t1")
+        banks = [gather(0, cross_t0), gather(1, cross_t0)]
+        x_grouped = transpose_rows(stage_half, halves(x_rows), 0, False)
+        centred = centre(0, banks[0])
+        x_q1 = quantise(x_grouped, "x1")
+        planes0 = value_products(x_q1, 0, False)
+        banks.append(gather(2, cross_t0))
+        planes1 = value_products(x_q1, 1, False)
+        previous, centred = centred, centre(1, banks[1])
+        finish(0, previous)
+        value_quantise(planes0, val_q1, 0)
+        banks.append(gather(3, cross_t0))
+        previous, centred = centred, centre(2, banks[2])
+        value_quantise(planes1, val_q1, 1)
+        finish(1, previous)
+        cross_products(val_q1, cross_t1, range(TILES), False)
+        previous, centred = centred, centre(3, banks[3])
+        finish(2, previous)
+        for t in range(HALF_TILES, TILES):
+            banks.append(gather(t, cross_t1))
+            previous, centred = centred, centre(t, banks[t])
+            finish(t - 1, previous)
+        finish(TILES - 1, centred)

@@ -5,7 +5,6 @@ from concourse.masks import make_identity
 
 BF16 = mybir.dt.bfloat16
 F32 = mybir.dt.float32
-I32 = mybir.dt.int32
 U32 = mybir.dt.uint32
 U8 = mybir.dt.uint8
 FP8X4 = mybir.dt.float8_e4m3fn_x4
@@ -17,11 +16,11 @@ SIZE = 1024
 PACK = 4
 PASSES = SIZE // (P * PACK)
 TILES = SIZE // P
-PAIRS = TILES // 2
+PAIR = 2
+PAIRS = TILES // PAIR
+ROWS = PAIR * P
 HALF = 512
-HALF_TILES = HALF // P
-BANK_BLOCKS = HALF // P
-VECTOR_TURN = 4
+BLOCKS = HALF // P
 EPS = 1e-5
 
 FLOPS = 2 * 2 * SIZE * SIZE * SIZE
@@ -33,7 +32,7 @@ def tile_efficientfusionlayer_pb_kernel(
     nc = tc.nc
 
     def batch_pairs(matrix):
-        view = matrix.rearrange("(p j e) d -> p j e d", j=PAIRS, e=2)
+        view = matrix.rearrange("(p j e) d -> p j e d", j=PAIRS, e=PAIR)
         return [view[:, j] for j in range(PAIRS)]
 
     x_view, feat_view, own_view = [batch_pairs(m) for m in (other_self, feat, own_self)]
@@ -41,105 +40,97 @@ def tile_efficientfusionlayer_pb_kernel(
     wv_rows = Wv.rearrange("(c p t) d -> p c t d", c=PASSES, t=PACK)
     wv_view = [wv_rows[:, j // 2, 2 * (j % 2) : 2 * (j % 2) + 2] for j in range(PAIRS)]
     bv_view = bv.rearrange("(c p t) -> p c t", c=PASSES, t=PACK)
-    wo_rows = Wo.rearrange("(j e p) v -> p j e v", j=PAIRS, e=2)
+    wo_rows = Wo.rearrange("(j e p) v -> p j e v", j=PAIRS, e=PAIR)
     wo_view = [wo_rows[:, j] for j in range(PAIRS)]
-    bo_view = bo.rearrange("(i p) -> p i", p=P)
+    by_partition = "(i p) -> p i"
 
     with ExitStack() as pools:
         const = pools.enter_context(tc.tile_pool(name="const", bufs=1))
         keep = pools.enter_context(tc.tile_pool(name="keep", bufs=1))
-        weight_rows = pools.enter_context(tc.tile_pool(name="weight_rows", bufs=6))
-        stage_one = pools.enter_context(tc.tile_pool(name="stage_one", bufs=4))
-        stage_half = pools.enter_context(tc.tile_pool(name="stage_half", bufs=1))
+        stage = pools.enter_context(tc.tile_pool(name="stage", bufs=3))
         work = pools.enter_context(tc.tile_pool(name="work", bufs=2))
-        normed = pools.enter_context(tc.tile_pool(name="normed", bufs=3))
-        small = pools.enter_context(tc.tile_pool(name="small", bufs=3))
+        lines = pools.enter_context(tc.tile_pool(name="lines", bufs=3))
+        small = pools.enter_context(tc.tile_pool(name="small", bufs=4))
         psum_chain = pools.enter_context(tc.psum_pool(name="psum_chain", bufs=4))
         psum_back = pools.enter_context(tc.psum_pool(name="psum_back", bufs=4))
 
-        def load_pair(pool, view, j, name):
-            rows = pool.tile([P, 2, SIZE], BF16, tag=name)
+        def load_pair(view, j, name):
+            rows = keep.tile([P, PAIR, SIZE], BF16, name="%s%d" % (name, j))
             nc.sync.dma_start(out=rows[:], in_=view[j])
             return rows
 
-        def empty_bank(turn, out_ap, bank, scale, bias_col):
-            if turn % VECTOR_TURN == VECTOR_TURN - 1:
-                nc.vector.tensor_scalar(
-                    out=out_ap, in0=bank, scalar1=scale, scalar2=bias_col, op0=ALU.mult, op1=ALU.add
-                )
-            else:
-                nc.scalar.activation(
-                    out=out_ap, in_=bank, func=ACT.Identity, bias=bias_col, scale=scale
-                )
+        def load_column(name, vector):
+            column = const.tile([P, TILES], BF16, name=name + "_raw")
+            with nc.allow_non_contiguous_dma(reason="1024 values, one to a partition"):
+                nc.sync.dma_start(out=column[:], in_=vector.rearrange("(i p) -> p i", p=P))
+            return column
 
-        norm_rows = const.tile([P, 2, SIZE], BF16)
-        nc.vector.memset(norm_rows[:].bitcast(I32), 0)
-        nc.sync.dma_start(out=norm_rows[0:1, 0, :], in_=g.unsqueeze(0))
-        nc.sync.dma_start(out=norm_rows[0:1, 1, :], in_=be.unsqueeze(0))
+        x_rows = [load_pair(x_view, 0, "x")]
+        wv_pairs = [load_pair(wv_view, j, "wv") for j in range(PAIRS)]
         bv_raw = const.tile([P, TILES], BF16)
         nc.sync.dma_start(out=bv_raw[:].rearrange("p (c t) -> p c t", t=PACK), in_=bv_view)
-        bo_raw = const.tile([P, TILES], BF16)
-        with nc.allow_non_contiguous_dma(reason="1024 bias values, one to a partition"):
-            nc.sync.dma_start(out=bo_raw[:], in_=bo_view)
-        x_rows = [load_pair(weight_rows, x_view, k, "rows") for k in range(2)]
+        wo_pairs = [load_pair(wo_view, j, "wo") for j in range(PAIRS)]
+        bo_raw = load_column("bo", bo)
+        x_rows.append(load_pair(x_view, 1, "x"))
+        norm_raw = [load_column("g", g), load_column("be", be)]
+        resid = [(load_pair(feat_view, 0, "feat"), load_pair(own_view, 0, "own"))]
+        for j in range(1, PAIRS):
+            if j + 1 < PAIRS:
+                x_rows.append(load_pair(x_view, j + 1, "x"))
+            resid.append((load_pair(feat_view, j, "feat"), load_pair(own_view, j, "own")))
 
         ident = const.tile([P, P], F32)
         make_identity(nc, ident[:])
         ident_bf = const.tile([P, P], BF16)
         make_identity(nc, ident_bf[:])
-        ones_bf = const.tile([P, P], BF16)
-        nc.vector.memset(ones_bf[:], 1.0)
+        half_ident_bf = const.tile([P, P], BF16)
+        nc.vector.tensor_scalar(
+            out=half_ident_bf[:], in0=ident_bf[:], scalar1=0.5, scalar2=None, op0=ALU.mult
+        )
         eps_col = const.tile([P, 1], F32)
         nc.vector.memset(eps_col[:], EPS)
         warm = const.tile([P, 1], F32)
         nc.scalar.activation(out=warm[:], in_=eps_col[:], func=ACT.Sqrt)
-
-
-        def convert_biases():
-            nc.vector.tensor_copy(out=bv_col[:], in_=bv_raw[:])
-            nc.vector.tensor_scalar(
-                out=half_bo_col[:], in0=bo_raw[:], scalar1=0.5, scalar2=None, op0=ALU.mult
-            )
-
-        def spread_norm_rows():
-            for v in range(2):
-                for k in range(2):
-                    cols = slice(k * HALF, (k + 1) * HALF)
-                    spread = psum_back.tile([P, HALF], F32, tag="back")
-                    nc.tensor.matmul(
-                        out=spread[:], lhsT=ones_bf[:], rhs=norm_rows[:, v, cols], start=True, stop=True
-                    )
-                    nc.vector.tensor_copy(out=norm_all[:, v, cols], in_=spread[:])
-
-        bv_col = const.tile([P, TILES], F32)
         half_bo_col = const.tile([P, TILES], F32)
         norm_all = const.tile([P, 2, SIZE], BF16)
         g_all = norm_all[:, 0, :]
         be_all = norm_all[:, 1, :]
 
-        def transpose_rows(stage, row_tiles, first_turn, vector_helps):
-            n_rows = P * len(row_tiles)
-            grouped = stage.tile([P, PASSES, n_rows, PACK], BF16, tag="grouped", align_bytes=64)
-            grouped_words = grouped[:].bitcast(F32)
-            for n, rows in enumerate(row_tiles):
-                words = rows.bitcast(F32)
+        def spread_norm_rows():
+            for v in range(2):
+                spread = psum_back.tile([P, TILES, P], BF16, tag="back")
+                for i in range(TILES):
+                    repeated = norm_raw[v][:, i : i + 1].to_broadcast([P, P])
+                    nc.tensor.transpose(spread[:, i, :], repeated, ident_bf[:])
+                nc.scalar.copy(out=norm_all[:, v, :], in_=spread[:].rearrange("p i n -> p (i n)"))
+
+        def turn(rows):
+            banks = []
+            for n in range(PAIR):
+                words = rows[:, n, :].bitcast(F32)
                 turned = psum_chain.tile([P, PASSES, 2, P], F32, tag="chain")
                 for c in range(PASSES):
                     for u in range(2):
                         every_second = words[:, 2 * P * c + u : 2 * P * (c + 1) : 2]
                         nc.tensor.transpose(turned[:, c, u, :], every_second, ident[:])
+                banks.append(turned)
+            return banks
+
+        def empty_turned(banks, vector_tiles):
+            grouped = stage.tile([P, PASSES, ROWS, PACK], BF16, tag="grouped", align_bytes=64)
+            grouped_words = grouped[:].bitcast(F32)
+            for n in range(PAIR):
                 copy_out = grouped_words[:, :, n * P : (n + 1) * P, :]
-                copy_in = turned[:].rearrange("p c u r -> p c r u")
-                if vector_helps and (first_turn + n) % VECTOR_TURN == VECTOR_TURN - 1:
+                copy_in = banks[n][:].rearrange("p c u r -> p c r u")
+                if n in vector_tiles:
                     nc.vector.tensor_copy(out=copy_out, in_=copy_in)
                 else:
                     nc.scalar.copy(out=copy_out, in_=copy_in)
             return grouped
 
         def quantise(grouped, name):
-            n_rows = grouped.shape[2]
-            codes = keep.tile([P, PASSES, n_rows], U32, name=name + "_codes", align_bytes=64)
-            scales = keep.tile([P, PASSES, n_rows], U8, name=name + "_scales", align_bytes=64)
+            codes = keep.tile([P, PASSES, ROWS], U32, name=name + "_codes", align_bytes=64)
+            scales = keep.tile([P, PASSES, ROWS], U8, name=name + "_scales", align_bytes=64)
             nc.vector.quantize_mx(
                 out=codes[:].rearrange("p c r -> p (c r)").bitcast(FP8X4),
                 scales=scales[:].rearrange("p c r -> p (c r)"),
@@ -147,103 +138,111 @@ def tile_efficientfusionlayer_pb_kernel(
             )
             return codes, scales
 
-        def mx_product(acc, stationary, moving):
+        def mx_product(acc, weights, i, moving):
+            codes, scales = weights[i // PAIR]
+            cols = slice((i % PAIR) * P, (i % PAIR + 1) * P)
             for c in range(PASSES):
                 nc.tensor.matmul_mx(
                     out=acc,
-                    lhsT=stationary[0][:, c, :].bitcast(FP8X4),
-                    lhsT_scale=stationary[1][:, c, :],
+                    lhsT=codes[:, c, cols].bitcast(FP8X4),
+                    lhsT_scale=scales[:, c, cols],
                     rhs=moving[0][:, c, :].bitcast(FP8X4),
                     rhs_scale=moving[1][:, c, :],
                     start=(c == 0),
                     stop=(c == PASSES - 1),
                 )
 
-        def quantise_weight(view, name, pairs, quantised, vector_helps):
-            waiting = None
-            for j in pairs:
-                rows = load_pair(weight_rows, view, j, "rows")
-                for e in range(2):
-                    grouped = transpose_rows(stage_one, [rows[:, e, :]], 2 * j + e, vector_helps)
-                    if waiting is not None:
-                        quantised.append(quantise(waiting, "%s%d" % (name, len(quantised))))
-                    waiting = grouped
-            quantised.append(quantise(waiting, "%s%d" % (name, len(quantised))))
+        def value_products(x_q, c, h, planes):
+            acc = psum_chain.tile([P, 2, ROWS], F32, tag="chain")
+            for k in range(2):
+                mx_product(acc[:, k, :], wv_q, PACK * c + 2 * h + k, x_q)
+            for k in range(2):
+                t = 2 * h + k
+                nc.scalar.activation(
+                    out=planes[:, t, :],
+                    in_=acc[:, k, :],
+                    func=ACT.Identity,
+                    bias=bv_raw[:, PACK * c + t : PACK * c + t + 1],
+                    scale=1.0,
+                )
 
-        def value_products(x_q, c, vector_helps):
-            planes = work.tile([P, PACK, HALF], BF16, tag="planes")
-            for t in range(PACK):
-                acc = psum_chain.tile([P, HALF], F32, tag="chain")
-                mx_product(acc[:], wv_q[PACK * c + t], x_q)
-                bias_col = bv_col[:, PACK * c + t : PACK * c + t + 1]
-                empty_bank(t if vector_helps else 0, planes[:, t, :], acc[:], 1.0, bias_col)
-            return planes
-
-        def value_quantise(planes, val_q, c):
-            grouped = work.tile([P, HALF, PACK], BF16, tag="val_grouped", align_bytes=64)
+        def interleave(planes):
+            grouped = work.tile([P, ROWS, PACK], BF16, tag="val_grouped", align_bytes=64)
             nc.vector.tensor_copy(
                 out=grouped[:].rearrange("p (n i) t -> p n t i", i=4),
                 in_=planes[:].rearrange("p t (n i) -> p n t i", i=4),
             )
+            return grouped
+
+        def new_val(j):
+            codes = keep.tile([P, PASSES, ROWS], U32, name="val%d_codes" % j, align_bytes=64)
+            scales = keep.tile([P, PASSES, ROWS], U8, name="val%d_scales" % j, align_bytes=64)
+            return codes, scales
+
+        def value_quantise(grouped, val_q, c):
             nc.vector.quantize_mx(
                 out=val_q[0][:, c, :].bitcast(FP8X4),
                 scales=val_q[1][:, c, :],
                 in_=grouped[:].rearrange("p n t -> p (n t)"),
             )
 
-        def new_val(h):
-            codes = keep.tile([P, PASSES, HALF], U32, name="val%d_codes" % h, align_bytes=64)
-            scales = keep.tile([P, PASSES, HALF], U8, name="val%d_scales" % h, align_bytes=64)
-            return codes, scales
-
-        def cross_products(val_q, cross_t, tiles, vector_helps):
-            for i in tiles:
-                acc = psum_chain.tile([P, HALF], F32, tag="chain")
-                mx_product(acc[:], wo_q[i], val_q)
-                empty_bank(
-                    i if vector_helps else 0, cross_t[:, i, :], acc[:], 0.5, half_bo_col[:, i : i + 1]
+        def cross_products(val_q, h, cross_t):
+            acc = psum_chain.tile([P, 2, ROWS], F32, tag="chain")
+            for k in range(2):
+                mx_product(acc[:, k, :], wo_q, 2 * h + k, val_q)
+            for k in range(2):
+                i = 2 * h + k
+                nc.scalar.activation(
+                    out=cross_t[:, i, :],
+                    in_=acc[:, k, :],
+                    func=ACT.Identity,
+                    bias=half_bo_col[:, i : i + 1],
+                    scale=0.5,
                 )
 
         def gather(t, cross_t):
-            first = (t % HALF_TILES) * P
-            feat_rows = resid[t // 2][0][:, t % 2, :]
+            feat_rows, own_rows = [rows[:, t % PAIR, :] for rows in resid[t // PAIR]]
+            first = (t % PAIR) * P
             banks = []
             for k in range(2):
-                back = psum_back.tile([P, BANK_BLOCKS, P], F32, tag="back")
+                cols = slice(k * HALF, (k + 1) * HALF)
+                back = psum_back.tile([P, BLOCKS, P], F32, tag="back")
+                whole = back[:].rearrange("p n r -> p (n r)")
                 nc.tensor.matmul(
-                    out=back[:].rearrange("p n r -> p (n r)"),
-                    lhsT=ident_bf[:],
-                    rhs=feat_rows[:, k * HALF : (k + 1) * HALF],
-                    start=True,
-                    stop=False,
+                    out=whole, lhsT=ident_bf[:], rhs=feat_rows[:, cols], start=True, stop=False
                 )
-                for n in range(BANK_BLOCKS):
+                if k == 0:
+                    nc.tensor.matmul(
+                        out=whole, lhsT=half_ident_bf[:], rhs=own_rows[:, cols], start=False, stop=False
+                    )
+                for n in range(BLOCKS):
                     nc.tensor.matmul(
                         out=back[:, n, :],
-                        lhsT=cross_t[:, BANK_BLOCKS * k + n, first : first + P],
+                        lhsT=cross_t[:, BLOCKS * k + n, first : first + P],
                         rhs=ident[:],
                         is_transpose=True,
                         start=False,
-                        stop=(n == BANK_BLOCKS - 1),
+                        stop=(n == BLOCKS - 1),
                     )
-                banks.append(back)
+                banks.append(whole)
             return banks
 
-        def centre(t, banks):
-            own_rows = resid[t // 2][1][:, t % 2, :]
-            y = work.tile([P, SIZE], F32, tag="y")
+        def empty_gathered(t, banks):
+            own_rows = resid[t // PAIR][1][:, t % PAIR, :]
+            y = lines.tile([P, SIZE], F32, tag="y")
             sums = small.tile([P, 2], F32, tag="sums")
-            for k in range(2):
-                cols = slice(k * HALF, (k + 1) * HALF)
-                nc.vector.scalar_tensor_tensor(
-                    out=y[:, cols],
-                    in0=own_rows[:, cols],
-                    scalar=0.5,
-                    in1=banks[k][:].rearrange("p n r -> p (n r)"),
-                    op0=ALU.mult,
-                    op1=ALU.add,
-                    accum_out=sums[:, k : k + 1],
-                )
+            nc.scalar.activation(
+                out=y[:, :HALF], in_=banks[0], func=ACT.Identity, accum_out=sums[:, 0:1]
+            )
+            nc.vector.scalar_tensor_tensor(
+                out=y[:, HALF:],
+                in0=own_rows[:, HALF:],
+                scalar=0.5,
+                in1=banks[1],
+                op0=ALU.mult,
+                op1=ALU.add,
+                accum_out=sums[:, 1:2],
+            )
             neg_mean = small.tile([P, 1], F32, tag="neg_mean")
             nc.vector.tensor_scalar(
                 out=neg_mean[:],
@@ -253,6 +252,9 @@ def tile_efficientfusionlayer_pb_kernel(
                 op0=ALU.add,
                 op1=ALU.mult,
             )
+            return y, neg_mean
+
+        def spread_of(y, neg_mean):
             squares = work.tile([P, SIZE], BF16, tag="squares")
             sum_sq = small.tile([P, 1], F32, tag="sum_sq")
             nc.scalar.activation(
@@ -267,14 +269,16 @@ def tile_efficientfusionlayer_pb_kernel(
             nc.scalar.activation(
                 out=std[:], in_=sum_sq[:], func=ACT.Sqrt, bias=eps_col[:], scale=1.0 / SIZE
             )
-            result = normed.tile([P, SIZE], F32, tag="result")
+            return std
+
+        def centre(y, neg_mean):
+            result = lines.tile([P, SIZE], F32, tag="result")
             nc.vector.scalar_tensor_tensor(
                 out=result[:], in0=y[:], scalar=neg_mean[:], in1=g_all, op0=ALU.add, op1=ALU.mult
             )
-            return result, std
+            return result
 
-        def finish(t, centred):
-            result, std = centred
+        def finish(t, result, std):
             rstd = small.tile([P, 1], F32, tag="rstd")
             nc.vector.reciprocal(out=rstd[:], in_=std[:])
             nc.vector.scalar_tensor_tensor(
@@ -282,53 +286,68 @@ def tile_efficientfusionlayer_pb_kernel(
             )
             nc.sync.dma_start(out=out_view[:, t, :], in_=result[:])
 
-        def load_resid(j):
-            return load_pair(keep, feat_view, j, "feat%d" % j), load_pair(keep, own_view, j, "own%d" % j)
+        SECOND = (1,)
 
-        def halves(rows_list):
-            return [rows[:, e, :] for rows in rows_list for e in range(2)]
+        def turned(rows, vector_tiles, name):
+            return quantise(empty_turned(turn(rows), vector_tiles), name)
 
-        x_grouped = transpose_rows(stage_half, halves(x_rows), 0, True)
-        x_q0 = quantise(x_grouped, "x0")
-        convert_biases()
-        wv_q = []
-        quantise_weight(wv_view, "wv", range(0, 2), wv_q, True)
-        val_q0 = new_val(0)
-        wo_q = []
-        planes0 = value_products(x_q0, 0, True)
-        quantise_weight(wv_view, "wv", range(2, 4), wv_q, True)
-        value_quantise(planes0, val_q0, 0)
-        planes1 = value_products(x_q0, 1, True)
-        quantise_weight(wo_view, "wo", range(0, 1), wo_q, False)
-        value_quantise(planes1, val_q0, 1)
-        quantise_weight(wo_view, "wo", range(1, 4), wo_q, False)
-        x_rows = [load_pair(weight_rows, x_view, 2 + k, "rows") for k in range(2)]
-        resid = [load_resid(j) for j in range(PAIRS)]
-        spread_norm_rows()
-        cross_t0 = keep.tile([P, TILES, HALF], F32, name="cross_t0")
-        cross_products(val_q0, cross_t0, range(TILES), True)
+        def new_planes():
+            return work.tile([P, PACK, ROWS], BF16, name="planes")
 
-        val_q1 = new_val(1)
-        cross_t1 = keep.tile([P, TILES, HALF], F32, name="cross_t1")
-        banks = [gather(0, cross_t0), gather(1, cross_t0)]
-        x_grouped = transpose_rows(stage_half, halves(x_rows), 0, False)
-        centred = centre(0, banks[0])
-        x_q1 = quantise(x_grouped, "x1")
-        planes0 = value_products(x_q1, 0, False)
-        banks.append(gather(2, cross_t0))
-        planes1 = value_products(x_q1, 1, False)
-        previous, centred = centred, centre(1, banks[1])
-        finish(0, previous)
-        value_quantise(planes0, val_q1, 0)
-        banks.append(gather(3, cross_t0))
-        previous, centred = centred, centre(2, banks[2])
-        value_quantise(planes1, val_q1, 1)
-        finish(1, previous)
-        cross_products(val_q1, cross_t1, range(TILES), False)
-        previous, centred = centred, centre(3, banks[3])
-        finish(2, previous)
-        for t in range(HALF_TILES, TILES):
-            banks.append(gather(t, cross_t1))
-            previous, centred = centred, centre(t, banks[t])
-            finish(t - 1, previous)
-        finish(TILES - 1, centred)
+        with tc.manual_schedule():
+            x_q = [turned(x_rows[0], SECOND, "x0")]
+            wv_q = [turned(wv_pairs[j], SECOND if j % 2 else (), "wv%d" % j) for j in range(2)]
+            val_q = [new_val(j) for j in range(PAIRS)]
+            waiting = []
+            def weight(pairs, j, name, quantised):
+                grouped = empty_turned(turn(pairs[j]), SECOND)
+                quantised.append(quantise(grouped, "%s%d" % (name, j)))
+            weight(wv_pairs, 2, "wv", wv_q)
+            weight(wv_pairs, 3, "wv", wv_q)
+            wo_q = []
+            planes = [new_planes(), new_planes()]
+            value_products(x_q[0], 0, 0, planes[0])
+            value_products(x_q[0], 0, 1, planes[0])
+            weight(wo_pairs, 0, "wo", wo_q)
+            value_quantise(interleave(planes[0]), val_q[0], 0)
+            value_products(x_q[0], 1, 0, planes[1])
+            value_products(x_q[0], 1, 1, planes[1])
+            weight(wo_pairs, 1, "wo", wo_q)
+            value_quantise(interleave(planes[1]), val_q[0], 1)
+            weight(wo_pairs, 2, "wo", wo_q)
+            weight(wo_pairs, 3, "wo", wo_q)
+            nc.vector.tensor_scalar(
+                out=half_bo_col[:], in0=bo_raw[:], scalar1=0.5, scalar2=None, op0=ALU.mult
+            )
+            x_q.append(turned(x_rows[1], SECOND, "x1"))
+            spread_norm_rows()
+
+            ready = []
+            for j in range(PAIRS + 1):
+                stds, results = [], []
+                if j < PAIRS:
+                    cross_t = work.tile([P, TILES, ROWS], F32, tag="cross_t")
+                for h in range(4):
+                    if ready and h < PAIR:
+                        t, y, neg_mean = ready[h]
+                        stds.append(spread_of(y, neg_mean))
+                        results.append(centre(y, neg_mean))
+                    if j < PAIRS:
+                        cross_products(val_q[j], h, cross_t)
+                    if ready and h >= PAIR:
+                        finish(ready[h - PAIR][0], results[h - PAIR], stds[h - PAIR])
+                if j == PAIRS:
+                    continue
+                if j + 1 < PAIRS:
+                    planes = [new_planes(), new_planes()]
+                    for c in range(PASSES):
+                        for h in range(2):
+                            value_products(x_q[j + 1], c, h, planes[c])
+                        value_quantise(interleave(planes[c]), val_q[j + 1], c)
+                if j + 2 < PAIRS:
+                    banks = turn(x_rows[j + 2])
+                gathered = [gather(t, cross_t) for t in (PAIR * j, PAIR * j + 1)]
+                ready = [(PAIR * j,) + empty_gathered(PAIR * j, gathered[0])]
+                if j + 2 < PAIRS:
+                    x_q.append(quantise(empty_turned(banks, SECOND), "x%d" % (j + 2)))
+                ready.append((PAIR * j + 1,) + empty_gathered(PAIR * j + 1, gathered[1]))

@@ -49,8 +49,8 @@ def tile_efficientfusionlayer_pb_kernel(
         keep = pools.enter_context(tc.tile_pool(name="keep", bufs=1))
         stage = pools.enter_context(tc.tile_pool(name="stage", bufs=3))
         work = pools.enter_context(tc.tile_pool(name="work", bufs=2))
-        lines = pools.enter_context(tc.tile_pool(name="lines", bufs=3))
-        small = pools.enter_context(tc.tile_pool(name="small", bufs=4))
+        lines = pools.enter_context(tc.tile_pool(name="lines", bufs=4))
+        small = pools.enter_context(tc.tile_pool(name="small", bufs=6))
         psum_chain = pools.enter_context(tc.psum_pool(name="psum_chain", bufs=4))
         psum_back = pools.enter_context(tc.psum_pool(name="psum_back", bufs=4))
 
@@ -90,7 +90,7 @@ def tile_efficientfusionlayer_pb_kernel(
         eps_col = const.tile([P, 1], F32)
         nc.vector.memset(eps_col[:], EPS)
         warm = const.tile([P, 1], F32)
-        nc.scalar.activation(out=warm[:], in_=eps_col[:], func=ACT.Sqrt)
+        nc.scalar.activation(out=warm[:], in_=eps_col[:], func=ACT.Abs_reciprocal_sqrt)
         half_bo_col = const.tile([P, TILES], F32)
         norm_all = const.tile([P, 2, SIZE], BF16)
         g_all = norm_all[:, 0, :]
@@ -116,16 +116,13 @@ def tile_efficientfusionlayer_pb_kernel(
                 banks.append(turned)
             return banks
 
-        def empty_turned(banks, vector_tiles):
+        def empty_turned(banks):
             grouped = stage.tile([P, PASSES, ROWS, PACK], BF16, tag="grouped", align_bytes=64)
             grouped_words = grouped[:].bitcast(F32)
             for n in range(PAIR):
                 copy_out = grouped_words[:, :, n * P : (n + 1) * P, :]
                 copy_in = banks[n][:].rearrange("p c u r -> p c r u")
-                if n in vector_tiles:
-                    nc.vector.tensor_copy(out=copy_out, in_=copy_in)
-                else:
-                    nc.scalar.copy(out=copy_out, in_=copy_in)
+                nc.scalar.copy(out=copy_out, in_=copy_in)
             return grouped
 
         def quantise(grouped, name):
@@ -138,7 +135,7 @@ def tile_efficientfusionlayer_pb_kernel(
             )
             return codes, scales
 
-        def mx_product(acc, weights, i, moving):
+        def mx_product(acc, weights, i, moving, rows=slice(0, ROWS)):
             codes, scales = weights[i // PAIR]
             cols = slice((i % PAIR) * P, (i % PAIR + 1) * P)
             for c in range(PASSES):
@@ -146,33 +143,23 @@ def tile_efficientfusionlayer_pb_kernel(
                     out=acc,
                     lhsT=codes[:, c, cols].bitcast(FP8X4),
                     lhsT_scale=scales[:, c, cols],
-                    rhs=moving[0][:, c, :].bitcast(FP8X4),
-                    rhs_scale=moving[1][:, c, :],
+                    rhs=moving[0][:, c, rows].bitcast(FP8X4),
+                    rhs_scale=moving[1][:, c, rows],
                     start=(c == 0),
                     stop=(c == PASSES - 1),
                 )
 
-        def value_products(x_q, c, h, planes):
-            acc = psum_chain.tile([P, 2, ROWS], F32, tag="chain")
-            for k in range(2):
-                mx_product(acc[:, k, :], wv_q, PACK * c + 2 * h + k, x_q)
-            for k in range(2):
-                t = 2 * h + k
-                nc.scalar.activation(
-                    out=planes[:, t, :],
-                    in_=acc[:, k, :],
-                    func=ACT.Identity,
-                    bias=bv_raw[:, PACK * c + t : PACK * c + t + 1],
-                    scale=1.0,
-                )
-
-        def interleave(planes):
-            grouped = work.tile([P, ROWS, PACK], BF16, tag="val_grouped", align_bytes=64)
-            nc.vector.tensor_copy(
-                out=grouped[:].rearrange("p (n i) t -> p n t i", i=4),
-                in_=planes[:].rearrange("p t (n i) -> p n t i", i=4),
+        def value_direct(x_q, c, e, grouped):
+            acc = psum_chain.tile([P, PACK, P], F32, tag="chain")
+            for t in range(PACK):
+                mx_product(acc[:, t, :], wv_q, PACK * c + t, x_q, slice(e * P, (e + 1) * P))
+            bias = bv_raw[:, PACK * c : PACK * (c + 1)].unsqueeze(1).to_broadcast([P, P, PACK])
+            nc.vector.tensor_tensor(
+                out=grouped[:, e * P : (e + 1) * P, :],
+                in0=acc[:].rearrange("p t n -> p n t"),
+                in1=bias,
+                op=ALU.add,
             )
-            return grouped
 
         def new_val(j):
             codes = keep.tile([P, PASSES, ROWS], U32, name="val%d_codes" % j, align_bytes=64)
@@ -186,19 +173,29 @@ def tile_efficientfusionlayer_pb_kernel(
                 in_=grouped[:].rearrange("p n t -> p (n t)"),
             )
 
-        def cross_products(val_q, h, cross_t):
+        def cross_products(val_q, h, cross_t, vector_helps):
             acc = psum_chain.tile([P, 2, ROWS], F32, tag="chain")
             for k in range(2):
                 mx_product(acc[:, k, :], wo_q, 2 * h + k, val_q)
             for k in range(2):
                 i = 2 * h + k
-                nc.scalar.activation(
-                    out=cross_t[:, i, :],
-                    in_=acc[:, k, :],
-                    func=ACT.Identity,
-                    bias=half_bo_col[:, i : i + 1],
-                    scale=0.5,
-                )
+                if vector_helps:
+                    nc.vector.tensor_scalar(
+                        out=cross_t[:, i, :],
+                        in0=acc[:, k, :],
+                        scalar1=0.5,
+                        scalar2=half_bo_col[:, i : i + 1],
+                        op0=ALU.mult,
+                        op1=ALU.add,
+                    )
+                else:
+                    nc.scalar.activation(
+                        out=cross_t[:, i, :],
+                        in_=acc[:, k, :],
+                        func=ACT.Identity,
+                        bias=half_bo_col[:, i : i + 1],
+                        scale=0.5,
+                    )
 
         def gather(t, cross_t):
             feat_rows, own_rows = [rows[:, t % PAIR, :] for rows in resid[t // PAIR]]
@@ -243,18 +240,17 @@ def tile_efficientfusionlayer_pb_kernel(
                 op1=ALU.add,
                 accum_out=sums[:, 1:2],
             )
-            neg_mean = small.tile([P, 1], F32, tag="neg_mean")
-            nc.vector.tensor_scalar(
-                out=neg_mean[:],
-                in0=sums[:, 0:1],
-                scalar1=sums[:, 1:2],
-                scalar2=-1.0 / SIZE,
-                op0=ALU.add,
-                op1=ALU.mult,
-            )
-            return y, neg_mean
+            return y, sums
 
-        def spread_of(y, neg_mean):
+        def mean_of(sums):
+            parts = small.tile([P, 2], F32, tag="parts")
+            neg_mean = small.tile([P, 1], F32, tag="neg_mean")
+            nc.scalar.activation(
+                out=parts[:], in_=sums[:], func=ACT.Identity, scale=-1.0 / SIZE, accum_out=neg_mean[:]
+            )
+            return neg_mean
+
+        def sum_squares(y, neg_mean):
             squares = work.tile([P, SIZE], BF16, tag="squares")
             sum_sq = small.tile([P, 1], F32, tag="sum_sq")
             nc.scalar.activation(
@@ -265,11 +261,18 @@ def tile_efficientfusionlayer_pb_kernel(
                 scale=1.0,
                 accum_out=sum_sq[:],
             )
-            std = small.tile([P, 1], F32, tag="std")
+            return sum_sq
+
+        def reciprocal_deviation(sum_sq):
+            rstd = small.tile([P, 1], F32, tag="rstd")
             nc.scalar.activation(
-                out=std[:], in_=sum_sq[:], func=ACT.Sqrt, bias=eps_col[:], scale=1.0 / SIZE
+                out=rstd[:],
+                in_=sum_sq[:],
+                func=ACT.Abs_reciprocal_sqrt,
+                bias=eps_col[:],
+                scale=1.0 / SIZE,
             )
-            return std
+            return rstd
 
         def centre(y, neg_mean):
             result = lines.tile([P, SIZE], F32, tag="result")
@@ -278,76 +281,86 @@ def tile_efficientfusionlayer_pb_kernel(
             )
             return result
 
-        def finish(t, result, std):
-            rstd = small.tile([P, 1], F32, tag="rstd")
-            nc.vector.reciprocal(out=rstd[:], in_=std[:])
+        def finish(t, result, rstd):
             nc.vector.scalar_tensor_tensor(
                 out=result[:], in0=result[:], scalar=rstd[:], in1=be_all, op0=ALU.mult, op1=ALU.add
             )
             nc.sync.dma_start(out=out_view[:, t, :], in_=result[:])
 
-        SECOND = (1,)
+        LAST = PAIRS - 1
 
-        def turned(rows, vector_tiles, name):
-            return quantise(empty_turned(turn(rows), vector_tiles), name)
-
-        def new_planes():
-            return work.tile([P, PACK, ROWS], BF16, name="planes")
+        def value_half(j, c):
+            grouped = work.tile([P, ROWS, PACK], BF16, tag="val_grouped", align_bytes=64)
+            for e in range(2):
+                value_direct(x_q[j], c, e, grouped)
+            return grouped
 
         with tc.manual_schedule():
-            x_q = [turned(x_rows[0], SECOND, "x0")]
-            wv_q = [turned(wv_pairs[j], SECOND if j % 2 else (), "wv%d" % j) for j in range(2)]
             val_q = [new_val(j) for j in range(PAIRS)]
-            waiting = []
-            def weight(pairs, j, name, quantised):
-                grouped = empty_turned(turn(pairs[j]), SECOND)
-                quantised.append(quantise(grouped, "%s%d" % (name, j)))
-            weight(wv_pairs, 2, "wv", wv_q)
-            weight(wv_pairs, 3, "wv", wv_q)
-            wo_q = []
-            planes = [new_planes(), new_planes()]
-            value_products(x_q[0], 0, 0, planes[0])
-            value_products(x_q[0], 0, 1, planes[0])
-            weight(wo_pairs, 0, "wo", wo_q)
-            value_quantise(interleave(planes[0]), val_q[0], 0)
-            value_products(x_q[0], 1, 0, planes[1])
-            value_products(x_q[0], 1, 1, planes[1])
-            weight(wo_pairs, 1, "wo", wo_q)
-            value_quantise(interleave(planes[1]), val_q[0], 1)
-            weight(wo_pairs, 2, "wo", wo_q)
-            weight(wo_pairs, 3, "wo", wo_q)
+            x_q, wv_q, wo_q = [], [], []
+            jobs = (
+                [(x_rows[0], "x0", x_q)]
+                + [(wv_pairs[j], "wv%d" % j, wv_q) for j in range(PAIRS)]
+                + [(wo_pairs[j], "wo%d" % j, wo_q) for j in range(PAIRS)]
+                + [(x_rows[1], "x1", x_q)]
+            )
+            waiting = None
+            mixed = None
+            for n, (rows, name, quantised) in enumerate(jobs):
+                grouped = empty_turned(turn(rows))
+                if mixed is not None:
+                    value_quantise(*mixed)
+                    mixed = None
+                if waiting is not None:
+                    waiting[2].append(quantise(*waiting[:2]))
+                waiting = (grouped, name, quantised)
+                if n in (4, 6):
+                    c = 0 if n == 4 else 1
+                    mixed = (value_half(0, c), val_q[0], c)
+            waiting[2].append(quantise(*waiting[:2]))
             nc.vector.tensor_scalar(
                 out=half_bo_col[:], in0=bo_raw[:], scalar1=0.5, scalar2=None, op0=ALU.mult
             )
-            x_q.append(turned(x_rows[1], SECOND, "x1"))
             spread_norm_rows()
 
-            ready = []
-            for j in range(PAIRS + 1):
-                stds, results = [], []
-                if j < PAIRS:
-                    cross_t = work.tile([P, TILES, ROWS], F32, tag="cross_t")
+            before = []
+            for j in range(PAIRS):
+                cross_t = work.tile([P, TILES, ROWS], F32, tag="cross_t")
+                results, squares, means, rstds = [], [], [], []
                 for h in range(4):
-                    if ready and h < PAIR:
-                        t, y, neg_mean = ready[h]
-                        stds.append(spread_of(y, neg_mean))
-                        results.append(centre(y, neg_mean))
-                    if j < PAIRS:
-                        cross_products(val_q[j], h, cross_t)
-                    if ready and h >= PAIR:
-                        finish(ready[h - PAIR][0], results[h - PAIR], stds[h - PAIR])
-                if j == PAIRS:
-                    continue
-                if j + 1 < PAIRS:
-                    planes = [new_planes(), new_planes()]
-                    for c in range(PASSES):
-                        for h in range(2):
-                            value_products(x_q[j + 1], c, h, planes[c])
-                        value_quantise(interleave(planes[c]), val_q[j + 1], c)
-                if j + 2 < PAIRS:
-                    banks = turn(x_rows[j + 2])
+                    if before and h == 0:
+                        means.append(mean_of(before[0][2]))
+                        squares.append(sum_squares(before[0][1], means[0]))
+                        results.append(centre(before[0][1], means[0]))
+                        means.append(mean_of(before[1][2]))
+                        results.append(centre(before[1][1], means[1]))
+                    if before and j == LAST and h == 2:
+                        squares.append(sum_squares(before[1][1], means[1]))
+                    cross_products(val_q[j], h, cross_t, j == LAST and h >= 2)
+                    if before and h == 0:
+                        rstds.append(reciprocal_deviation(squares[0]))
+                        if j < LAST:
+                            finish(before[0][0], results[0], rstds[0])
+                if before and j == LAST:
+                    finish(before[0][0], results[0], rstds[0])
+                if before and j < LAST:
+                    squares.append(sum_squares(before[1][1], means[1]))
+                if j < LAST:
+                    first = value_half(j + 1, 0)
+                if before:
+                    rstds.append(reciprocal_deviation(squares[1]))
+                    finish(before[1][0], results[1], rstds[1])
+                if j < LAST:
+                    second = value_half(j + 1, 1)
+                    value_quantise(first, val_q[j + 1], 0)
                 gathered = [gather(t, cross_t) for t in (PAIR * j, PAIR * j + 1)]
-                ready = [(PAIR * j,) + empty_gathered(PAIR * j, gathered[0])]
+                before = [(PAIR * j,) + empty_gathered(PAIR * j, gathered[0])]
+                if j < LAST:
+                    value_quantise(second, val_q[j + 1], 1)
+                before.append((PAIR * j + 1,) + empty_gathered(PAIR * j + 1, gathered[1]))
                 if j + 2 < PAIRS:
-                    x_q.append(quantise(empty_turned(banks, SECOND), "x%d" % (j + 2)))
-                ready.append((PAIR * j + 1,) + empty_gathered(PAIR * j + 1, gathered[1]))
+                    x_q.append(quantise(empty_turned(turn(x_rows[j + 2])), "x%d" % (j + 2)))
+            means = [mean_of(b[2]) for b in before]
+            results = [centre(b[1], m) for b, m in zip(before, means)]
+            for n, (t, y, sums) in enumerate(before):
+                finish(t, results[n], reciprocal_deviation(sum_squares(y, means[n])))

@@ -72,8 +72,12 @@ def tile_efficientfusionlayer_pb_kernel(
         wo_pairs = [load_pair(wo_view, j, "wo") for j in range(PAIRS)]
         bo_raw = load_column("bo", bo)
         x_rows.append(load_pair(x_view, 1, "x"))
-        norm_raw = [load_column("g", g), load_column("be", be)]
         resid = [(load_pair(feat_view, 0, "feat"), load_pair(own_view, 0, "own"))]
+        norm_all = const.tile([P, 2, SIZE], BF16)
+        for v, vector in enumerate((g, be)):
+            nc.sync.dma_start(out=norm_all[:, v, :], in_=vector.partition_broadcast(P))
+        g_all = norm_all[:, 0, :]
+        be_all = norm_all[:, 1, :]
         for j in range(1, PAIRS):
             if j + 1 < PAIRS:
                 x_rows.append(load_pair(x_view, j + 1, "x"))
@@ -92,17 +96,6 @@ def tile_efficientfusionlayer_pb_kernel(
         warm = const.tile([P, 1], F32)
         nc.scalar.activation(out=warm[:], in_=eps_col[:], func=ACT.Abs_reciprocal_sqrt)
         half_bo_col = const.tile([P, TILES], F32)
-        norm_all = const.tile([P, 2, SIZE], BF16)
-        g_all = norm_all[:, 0, :]
-        be_all = norm_all[:, 1, :]
-
-        def spread_norm_rows():
-            for v in range(2):
-                spread = psum_back.tile([P, TILES, P], BF16, tag="back")
-                for i in range(TILES):
-                    repeated = norm_raw[v][:, i : i + 1].to_broadcast([P, P])
-                    nc.tensor.transpose(spread[:, i, :], repeated, ident_bf[:])
-                nc.scalar.copy(out=norm_all[:, v, :], in_=spread[:].rearrange("p i n -> p (i n)"))
 
         def turn(rows):
             banks = []
@@ -321,7 +314,6 @@ def tile_efficientfusionlayer_pb_kernel(
             nc.vector.tensor_scalar(
                 out=half_bo_col[:], in0=bo_raw[:], scalar1=0.5, scalar2=None, op0=ALU.mult
             )
-            spread_norm_rows()
 
             before = []
             for j in range(PAIRS):

@@ -22,6 +22,7 @@ ROWS = PAIR * P
 HALF = 512
 BLOCKS = HALF // P
 EPS = 1e-5
+BO_ROW = 8
 
 FLOPS = 2 * 2 * SIZE * SIZE * SIZE
 
@@ -39,7 +40,6 @@ def tile_efficientfusionlayer_pb_kernel(
     out_view = out.rearrange("(p t) d -> p t d", t=TILES)
     wv_rows = Wv.rearrange("(c p t) d -> p c t d", c=PASSES, t=PACK)
     wv_view = [wv_rows[:, j // 2, 2 * (j % 2) : 2 * (j % 2) + 2] for j in range(PAIRS)]
-    bv_view = bv.rearrange("(c p t) -> p c t", c=PASSES, t=PACK)
     wo_rows = Wo.rearrange("(j e p) v -> p j e v", j=PAIRS, e=PAIR)
     wo_view = [wo_rows[:, j] for j in range(PAIRS)]
     by_partition = "(i p) -> p i"
@@ -59,18 +59,16 @@ def tile_efficientfusionlayer_pb_kernel(
             nc.sync.dma_start(out=rows[:], in_=view[j])
             return rows
 
-        def load_column(name, vector):
-            column = const.tile([P, TILES], BF16, name=name + "_raw")
-            with nc.allow_non_contiguous_dma(reason="1024 values, one to a partition"):
-                nc.sync.dma_start(out=column[:], in_=vector.rearrange("(i p) -> p i", p=P))
-            return column
-
+        bias_rows = const.tile([P, HALF], BF16)
+        nc.vector.memset(bias_rows[:].bitcast(U32), 0)
         x_rows = [load_pair(x_view, 0, "x")]
-        wv_pairs = [load_pair(wv_view, j, "wv") for j in range(PAIRS)]
-        bv_raw = const.tile([P, TILES], BF16)
-        nc.sync.dma_start(out=bv_raw[:].rearrange("p (c t) -> p c t", t=PACK), in_=bv_view)
+        wv_pairs = [load_pair(wv_view, j, "wv") for j in range(2)]
+        nc.sync.dma_start(out=bias_rows[0:PASSES, :], in_=bv.rearrange("(c v) -> c v", c=PASSES))
+        nc.sync.dma_start(
+            out=bias_rows[BO_ROW : BO_ROW + TILES, 0:P], in_=bo.rearrange("(i p) -> i p", p=P)
+        )
+        wv_pairs += [load_pair(wv_view, j, "wv") for j in range(2, PAIRS)]
         wo_pairs = [load_pair(wo_view, j, "wo") for j in range(PAIRS)]
-        bo_raw = load_column("bo", bo)
         x_rows.append(load_pair(x_view, 1, "x"))
         resid = [(load_pair(feat_view, 0, "feat"), load_pair(own_view, 0, "own"))]
         norm_all = const.tile([P, 2, SIZE], BF16)
@@ -95,7 +93,26 @@ def tile_efficientfusionlayer_pb_kernel(
         nc.vector.memset(eps_col[:], EPS)
         warm = const.tile([P, 1], F32)
         nc.scalar.activation(out=warm[:], in_=eps_col[:], func=ACT.Abs_reciprocal_sqrt)
+        bv_raw = const.tile([P, TILES], BF16)
         half_bo_col = const.tile([P, TILES], F32)
+
+        def turn_biases():
+            turned = psum_back.tile([P, PACK + 1, P], BF16, tag="back")
+            for t in range(PACK):
+                nc.tensor.transpose(turned[:, t, :], bias_rows[:, t::PACK], ident_bf[:])
+            nc.tensor.transpose(turned[:, PACK, :], bias_rows[:, 0:P], ident_bf[:])
+            nc.vector.tensor_copy(
+                out=bv_raw[:].rearrange("p (c t) -> p c t", t=PACK),
+                in_=turned[:, 0:PACK, 0:PASSES].rearrange("p t c -> p c t"),
+            )
+            nc.vector.tensor_scalar(
+                out=half_bo_col[:],
+                in0=turned[:, PACK, BO_ROW : BO_ROW + TILES],
+                scalar1=0.5,
+                scalar2=None,
+                op0=ALU.mult,
+            )
+
 
         def turn(rows):
             banks = []
@@ -307,13 +324,12 @@ def tile_efficientfusionlayer_pb_kernel(
                 if waiting is not None:
                     waiting[2].append(quantise(*waiting[:2]))
                 waiting = (grouped, name, quantised)
+                if n == 3:
+                    turn_biases()
                 if n in (4, 6):
                     c = 0 if n == 4 else 1
                     mixed = (value_half(0, c), val_q[0], c)
             waiting[2].append(quantise(*waiting[:2]))
-            nc.vector.tensor_scalar(
-                out=half_bo_col[:], in0=bo_raw[:], scalar1=0.5, scalar2=None, op0=ALU.mult
-            )
 
             before = []
             for j in range(PAIRS):

@@ -114,15 +114,21 @@ def tile_efficientfusionlayer_pb_kernel(
             )
 
 
-        def turn(rows):
+        def word_planes(rows):
+            return rows.bitcast(F32).rearrange("p (c w u) -> p c u w", c=PASSES, u=2)
+
+        def reorder(rows, copy):
+            ordered = stage.tile([P, PASSES, 2, P], F32, tag="ordered", bufs=4)
+            copy(out=ordered[:], in_=word_planes(rows))
+            return ordered[:]
+
+        def turn(planes_of_tiles):
             banks = []
-            for n in range(PAIR):
-                words = rows[:, n, :].bitcast(F32)
+            for planes in planes_of_tiles:
                 turned = psum_chain.tile([P, PASSES, 2, P], F32, tag="chain")
                 for c in range(PASSES):
                     for u in range(2):
-                        every_second = words[:, 2 * P * c + u : 2 * P * (c + 1) : 2]
-                        nc.tensor.transpose(turned[:, c, u, :], every_second, ident[:])
+                        nc.tensor.transpose(turned[:, c, u, :], planes[:, c, u, :], ident[:])
                 banks.append(turned)
             return banks
 
@@ -207,6 +213,9 @@ def tile_efficientfusionlayer_pb_kernel(
                         scale=0.5,
                     )
 
+        def scalar_banks(t):
+            return (0, 1) if t == TILES - 1 else (0,)
+
         def gather(t, cross_t):
             feat_rows, own_rows = [rows[:, t % PAIR, :] for rows in resid[t // PAIR]]
             first = (t % PAIR) * P
@@ -218,7 +227,7 @@ def tile_efficientfusionlayer_pb_kernel(
                 nc.tensor.matmul(
                     out=whole, lhsT=ident_bf[:], rhs=feat_rows[:, cols], start=True, stop=False
                 )
-                if k == 0:
+                if k in scalar_banks(t):
                     nc.tensor.matmul(
                         out=whole, lhsT=half_ident_bf[:], rhs=own_rows[:, cols], start=False, stop=False
                     )
@@ -238,18 +247,22 @@ def tile_efficientfusionlayer_pb_kernel(
             own_rows = resid[t // PAIR][1][:, t % PAIR, :]
             y = lines.tile([P, SIZE], F32, tag="y")
             sums = small.tile([P, 2], F32, tag="sums")
-            nc.scalar.activation(
-                out=y[:, :HALF], in_=banks[0], func=ACT.Identity, accum_out=sums[:, 0:1]
-            )
-            nc.vector.scalar_tensor_tensor(
-                out=y[:, HALF:],
-                in0=own_rows[:, HALF:],
-                scalar=0.5,
-                in1=banks[1],
-                op0=ALU.mult,
-                op1=ALU.add,
-                accum_out=sums[:, 1:2],
-            )
+            for k in range(2):
+                cols = slice(k * HALF, (k + 1) * HALF)
+                if k in scalar_banks(t):
+                    nc.scalar.activation(
+                        out=y[:, cols], in_=banks[k], func=ACT.Identity, accum_out=sums[:, k : k + 1]
+                    )
+                else:
+                    nc.vector.scalar_tensor_tensor(
+                        out=y[:, cols],
+                        in0=own_rows[:, cols],
+                        scalar=0.5,
+                        in1=banks[k],
+                        op0=ALU.mult,
+                        op1=ALU.add,
+                        accum_out=sums[:, k : k + 1],
+                    )
             return y, sums
 
         def mean_of(sums):
@@ -291,15 +304,22 @@ def tile_efficientfusionlayer_pb_kernel(
             )
             return result
 
-        def finish(t, result, rstd):
-            nc.vector.scalar_tensor_tensor(
-                out=result[:], in0=result[:], scalar=rstd[:], in1=be_all, op0=ALU.mult, op1=ALU.add
-            )
-            nc.sync.dma_start(out=out_view[:, t, :], in_=result[:])
+        def finish(t, result, rstd, pieces=1):
+            for k in range(pieces):
+                cols = slice(k * SIZE // pieces, (k + 1) * SIZE // pieces)
+                nc.vector.scalar_tensor_tensor(
+                    out=result[:, cols],
+                    in0=result[:, cols],
+                    scalar=rstd[:],
+                    in1=be_all[:, cols],
+                    op0=ALU.mult,
+                    op1=ALU.add,
+                )
+                nc.sync.dma_start(out=out_view[:, t, cols], in_=result[:, cols])
 
         LAST = PAIRS - 1
 
-        def value_half(j, c):
+        def value_start(j, c):
             grouped = work.tile([P, ROWS, PACK], BF16, tag="val_grouped", align_bytes=64)
             for e in range(2):
                 value_direct(x_q[j], c, e, grouped)
@@ -314,10 +334,20 @@ def tile_efficientfusionlayer_pb_kernel(
                 + [(wo_pairs[j], "wo%d" % j, wo_q) for j in range(PAIRS)]
                 + [(x_rows[1], "x1", x_q)]
             )
+
+            def begin(n):
+                first, second = [jobs[n][0][:, e, :] for e in range(PAIR)]
+                reordered = jobs[n][2] is not x_q
+                return word_planes(first), reorder(second, nc.vector.tensor_copy) if reordered else word_planes(second)
+
             waiting = None
             mixed = None
+            planes = begin(0)
             for n, (rows, name, quantised) in enumerate(jobs):
-                grouped = empty_turned(turn(rows))
+                banks = turn(planes)
+                if n + 1 < len(jobs):
+                    planes = begin(n + 1)
+                grouped = empty_turned(banks)
                 if mixed is not None:
                     value_quantise(*mixed)
                     mixed = None
@@ -328,47 +358,41 @@ def tile_efficientfusionlayer_pb_kernel(
                     turn_biases()
                 if n in (4, 6):
                     c = 0 if n == 4 else 1
-                    mixed = (value_half(0, c), val_q[0], c)
+                    mixed = (value_start(0, c), val_q[0], c)
             waiting[2].append(quantise(*waiting[:2]))
-
             before = []
             for j in range(PAIRS):
                 cross_t = work.tile([P, TILES, ROWS], F32, tag="cross_t")
-                results, squares, means, rstds = [], [], [], []
-                for h in range(4):
-                    if before and h == 0:
-                        means.append(mean_of(before[0][2]))
-                        squares.append(sum_squares(before[0][1], means[0]))
-                        results.append(centre(before[0][1], means[0]))
-                        means.append(mean_of(before[1][2]))
-                        results.append(centre(before[1][1], means[1]))
+                lag = 1 if j == LAST else 0
+                means, results, rstds = [], [], []
+                for h in range(TILES // 2):
+                    if lag <= h < lag + len(before):
+                        t, y, sums = before[h - lag]
+                        means.append(mean_of(sums))
+                        results.append(centre(y, means[-1]))
                     if before and j == LAST and h == 2:
-                        squares.append(sum_squares(before[1][1], means[1]))
-                    cross_products(val_q[j], h, cross_t, j == LAST and h >= 2)
-                    if before and h == 0:
-                        rstds.append(reciprocal_deviation(squares[0]))
-                        if j < LAST:
-                            finish(before[0][0], results[0], rstds[0])
-                if before and j == LAST:
-                    finish(before[0][0], results[0], rstds[0])
-                if before and j < LAST:
-                    squares.append(sum_squares(before[1][1], means[1]))
+                        rstds.append(reciprocal_deviation(sum_squares(before[0][1], means[0])))
+                    cross_products(val_q[j], h, cross_t, j == LAST and h == 3)
                 if j < LAST:
-                    first = value_half(j + 1, 0)
+                    first = value_start(j + 1, 0)
+                for n in range(len(rstds), len(before)):
+                    rstds.append(reciprocal_deviation(sum_squares(before[n][1], means[n])))
                 if before:
-                    rstds.append(reciprocal_deviation(squares[1]))
-                    finish(before[1][0], results[1], rstds[1])
+                    finish(before[0][0], results[0], rstds[0])
                 if j < LAST:
-                    second = value_half(j + 1, 1)
+                    second = value_start(j + 1, 1)
                     value_quantise(first, val_q[j + 1], 0)
-                gathered = [gather(t, cross_t) for t in (PAIR * j, PAIR * j + 1)]
-                before = [(PAIR * j,) + empty_gathered(PAIR * j, gathered[0])]
-                if j < LAST:
                     value_quantise(second, val_q[j + 1], 1)
-                before.append((PAIR * j + 1,) + empty_gathered(PAIR * j + 1, gathered[1]))
+                if before:
+                    finish(before[1][0], results[1], rstds[1])
                 if j + 2 < PAIRS:
-                    x_q.append(quantise(empty_turned(turn(x_rows[j + 2])), "x%d" % (j + 2)))
+                    planes = [reorder(x_rows[j + 2][:, e, :], nc.scalar.copy) for e in range(PAIR)]
+                tiles = [PAIR * j + n for n in range(PAIR)]
+                gathered = [gather(t, cross_t) for t in tiles]
+                before = [(t,) + empty_gathered(t, banks) for t, banks in zip(tiles, gathered)]
+                if j + 2 < PAIRS:
+                    x_q.append(quantise(empty_turned(turn(planes)), "x%d" % (j + 2)))
             means = [mean_of(b[2]) for b in before]
             results = [centre(b[1], m) for b, m in zip(before, means)]
             for n, (t, y, sums) in enumerate(before):
-                finish(t, results[n], reciprocal_deviation(sum_squares(y, means[n])))
+                finish(t, results[n], reciprocal_deviation(sum_squares(y, means[n])), pieces=2)

@@ -214,7 +214,7 @@ def tile_efficientfusionlayer_pb_kernel(
                     )
 
         def scalar_banks(t):
-            return (0, 1) if t == TILES - 1 else (0,)
+            return (0, 1) if t == TILES - PAIR else (0,)
 
         def gather(t, cross_t):
             feat_rows, own_rows = [rows[:, t % PAIR, :] for rows in resid[t // PAIR]]
@@ -231,17 +231,18 @@ def tile_efficientfusionlayer_pb_kernel(
                     nc.tensor.matmul(
                         out=whole, lhsT=half_ident_bf[:], rhs=own_rows[:, cols], start=False, stop=False
                     )
+                banks.append((back, whole))
+            for k in range(2):
                 for n in range(BLOCKS):
                     nc.tensor.matmul(
-                        out=back[:, n, :],
+                        out=banks[k][0][:, n, :],
                         lhsT=cross_t[:, BLOCKS * k + n, first : first + P],
                         rhs=ident[:],
                         is_transpose=True,
                         start=False,
                         stop=(n == BLOCKS - 1),
                     )
-                banks.append(whole)
-            return banks
+            return [whole for back, whole in banks]
 
         def empty_gathered(t, banks):
             own_rows = resid[t // PAIR][1][:, t % PAIR, :]
@@ -337,8 +338,7 @@ def tile_efficientfusionlayer_pb_kernel(
 
             def begin(n):
                 first, second = [jobs[n][0][:, e, :] for e in range(PAIR)]
-                reordered = jobs[n][2] is not x_q
-                return word_planes(first), reorder(second, nc.vector.tensor_copy) if reordered else word_planes(second)
+                return word_planes(first), reorder(second, nc.vector.tensor_copy) if n > 0 else word_planes(second)
 
             waiting = None
             mixed = None
@@ -356,7 +356,7 @@ def tile_efficientfusionlayer_pb_kernel(
                 waiting = (grouped, name, quantised)
                 if n == 3:
                     turn_biases()
-                if n in (4, 6):
+                if n in (4, 7):
                     c = 0 if n == 4 else 1
                     mixed = (value_start(0, c), val_q[0], c)
             waiting[2].append(quantise(*waiting[:2]))
@@ -395,4 +395,4 @@ def tile_efficientfusionlayer_pb_kernel(
             means = [mean_of(b[2]) for b in before]
             results = [centre(b[1], m) for b, m in zip(before, means)]
             for n, (t, y, sums) in enumerate(before):
-                finish(t, results[n], reciprocal_deviation(sum_squares(y, means[n])), pieces=2)
+                finish(t, results[n], reciprocal_deviation(sum_squares(y, means[n])), pieces=4)

@@ -74,10 +74,12 @@ def tile_efficientfusionlayer_pb_kernel(
         norm_all = const.tile([P, 2, SIZE], BF16)
         for v, vector in enumerate((g, be)):
             nc.sync.dma_start(out=norm_all[:, v, :], in_=vector.partition_broadcast(P))
+            if v == 0:
+                x_rows.append(load_pair(x_view, 2, "x"))
         g_all = norm_all[:, 0, :]
         be_all = norm_all[:, 1, :]
         for j in range(1, PAIRS):
-            if j + 1 < PAIRS:
+            if 2 < j + 1 < PAIRS:
                 x_rows.append(load_pair(x_view, j + 1, "x"))
             resid.append((load_pair(feat_view, j, "feat"), load_pair(own_view, j, "own")))
 
@@ -361,18 +363,19 @@ def tile_efficientfusionlayer_pb_kernel(
                     mixed = (value_start(0, c), val_q[0], c)
             waiting[2].append(quantise(*waiting[:2]))
             before = []
+            ahead = [], []
             for j in range(PAIRS):
                 cross_t = work.tile([P, TILES, ROWS], F32, tag="cross_t")
                 lag = 1 if j == LAST else 0
-                means, results, rstds = [], [], []
+                (means, results), rstds = ahead, []
                 for h in range(TILES // 2):
-                    if lag <= h < lag + len(before):
-                        t, y, sums = before[h - lag]
-                        means.append(mean_of(sums))
-                        results.append(centre(y, means[-1]))
-                    if before and j == LAST and h == 2:
+                    for n in range(len(means), len(before)):
+                        if lag + n <= h:
+                            means.append(mean_of(before[n][2]))
+                            results.append(centre(before[n][1], means[n]))
+                    if j == LAST and h == 2:
                         rstds.append(reciprocal_deviation(sum_squares(before[0][1], means[0])))
-                    cross_products(val_q[j], h, cross_t, j == LAST and h == 3)
+                    cross_products(val_q[j], h, cross_t, h == 3 and j in (1, LAST))
                 if j < LAST:
                     first = value_start(j + 1, 0)
                 for n in range(len(rstds), len(before)):
@@ -389,7 +392,12 @@ def tile_efficientfusionlayer_pb_kernel(
                     planes = [reorder(x_rows[j + 2][:, e, :], nc.scalar.copy) for e in range(PAIR)]
                 tiles = [PAIR * j + n for n in range(PAIR)]
                 gathered = [gather(t, cross_t) for t in tiles]
-                before = [(t,) + empty_gathered(t, banks) for t, banks in zip(tiles, gathered)]
+                before, ahead = [], ([], [])
+                for t, banks in zip(tiles, gathered):
+                    before.append((t,) + empty_gathered(t, banks))
+                    if t == 0:
+                        ahead[0].append(mean_of(before[0][2]))
+                        ahead[1].append(centre(before[0][1], ahead[0][0]))
                 if j + 2 < PAIRS:
                     x_q.append(quantise(empty_turned(turn(planes)), "x%d" % (j + 2)))
             means = [mean_of(b[2]) for b in before]

from contextlib import ExitStack

import concourse.mybir as mybir
from concourse.masks import make_identity

BF16 = mybir.dt.bfloat16
F32 = mybir.dt.float32
U32 = mybir.dt.uint32
U8 = mybir.dt.uint8
FP8X4 = mybir.dt.float8_e4m3fn_x4
ACT = mybir.ActivationFunctionType
ALU = mybir.AluOpType

P = 128
SIZE = 1024
PACK = 4
PASSES = SIZE // (P * PACK)
TILES = SIZE // P
PAIR = 2
PAIRS = TILES // PAIR
ROWS = PAIR * P
HALF = 512
BLOCKS = HALF // P
EPS = 1e-5
BO_ROW = 8

FLOPS = 2 * 2 * SIZE * SIZE * SIZE


def tile_efficientfusionlayer_pb_kernel(
    tc, feat, own_self, other_self, Wv, bv, Wo, bo, g, be, out
):
    nc = tc.nc

    def batch_pairs(matrix):
        view = matrix.rearrange("(p j e) d -> p j e d", j=PAIRS, e=PAIR)
        return [view[:, j] for j in range(PAIRS)]

    x_view, feat_view, own_view = [batch_pairs(m) for m in (other_self, feat, own_self)]
    out_view = out.rearrange("(p t) d -> p t d", t=TILES)
    wv_rows = Wv.rearrange("(c p t) d -> p c t d", c=PASSES, t=PACK)
    wv_view = [wv_rows[:, j // 2, 2 * (j % 2) : 2 * (j % 2) + 2] for j in range(PAIRS)]
    wo_rows = Wo.rearrange("(j e p) v -> p j e v", j=PAIRS, e=PAIR)
    wo_view = [wo_rows[:, j] for j in range(PAIRS)]
    by_partition = "(i p) -> p i"

    with ExitStack() as pools:
        const = pools.enter_context(tc.tile_pool(name="const", bufs=1))
        keep = pools.enter_context(tc.tile_pool(name="keep", bufs=1))
        stage = pools.enter_context(tc.tile_pool(name="stage", bufs=3))
        work = pools.enter_context(tc.tile_pool(name="work", bufs=2))
        lines = pools.enter_context(tc.tile_pool(name="lines", bufs=4))
        small = pools.enter_context(tc.tile_pool(name="small", bufs=6))
        psum_chain = pools.enter_context(tc.psum_pool(name="psum_chain", bufs=4))
        psum_back = pools.enter_context(tc.psum_pool(name="psum_back", bufs=4))

        def load_pair(view, j, name):
            rows = keep.tile([P, PAIR, SIZE], BF16, name="%s%d" % (name, j))
            nc.sync.dma_start(out=rows[:], in_=view[j])
            return rows

        bias_rows = const.tile([P, HALF], BF16)
        nc.vector.memset(bias_rows[:].bitcast(U32), 0)
        x_rows = [load_pair(x_view, 0, "x")]
        wv_pairs = [load_pair(wv_view, j, "wv") for j in range(2)]
        nc.sync.dma_start(out=bias_rows[0:PASSES, :], in_=bv.rearrange("(c v) -> c v", c=PASSES))
        nc.sync.dma_start(
            out=bias_rows[BO_ROW : BO_ROW + TILES, 0:P], in_=bo.rearrange("(i p) -> i p", p=P)
        )
        wv_pairs += [load_pair(wv_view, j, "wv") for j in range(2, PAIRS)]
        wo_pairs = [load_pair(wo_view, j, "wo") for j in range(PAIRS)]
        x_rows.append(load_pair(x_view, 1, "x"))
        resid = [(load_pair(feat_view, 0, "feat"), load_pair(own_view, 0, "own"))]
        norm_all = const.tile([P, 2, SIZE], BF16)
        for v, vector in enumerate((g, be)):
            nc.sync.dma_start(out=norm_all[:, v, :], in_=vector.partition_broadcast(P))
            if v == 0:
                x_rows.append(load_pair(x_view, 2, "x"))
        g_all = norm_all[:, 0, :]
        be_all = norm_all[:, 1, :]
        for j in range(1, PAIRS):
            if 2 < j + 1 < PAIRS:
                x_rows.append(load_pair(x_view, j + 1, "x"))
            resid.append((load_pair(feat_view, j, "feat"), load_pair(own_view, j, "own")))

        ident = const.tile([P, P], F32)
        make_identity(nc, ident[:])
        ident_bf = const.tile([P, P], BF16)
        make_identity(nc, ident_bf[:])
        half_ident_bf = const.tile([P, P], BF16)
        nc.vector.tensor_scalar(
            out=half_ident_bf[:], in0=ident_bf[:], scalar1=0.5, scalar2=None, op0=ALU.mult
        )
        eps_col = const.tile([P, 1], F32)
        nc.vector.memset(eps_col[:], EPS)
        warm = const.tile([P, 1], F32)
        nc.scalar.activation(out=warm[:], in_=eps_col[:], func=ACT.Abs_reciprocal_sqrt)
        bv_raw = const.tile([P, TILES], BF16)
        half_bo_col = const.tile([P, TILES], F32)

        def turn_biases():
            turned = psum_back.tile([P, PACK + 1, P], BF16, tag="back")
            for t in range(PACK):
                nc.tensor.transpose(turned[:, t, :], bias_rows[:, t::PACK], ident_bf[:])
            nc.tensor.transpose(turned[:, PACK, :], bias_rows[:, 0:P], ident_bf[:])
            nc.vector.tensor_copy(
                out=bv_raw[:].rearrange("p (c t) -> p c t", t=PACK),
                in_=turned[:, 0:PACK, 0:PASSES].rearrange("p t c -> p c t"),
            )
            nc.vector.tensor_scalar(
                out=half_bo_col[:],
                in0=turned[:, PACK, BO_ROW : BO_ROW + TILES],
                scalar1=0.5,
                scalar2=None,
                op0=ALU.mult,
            )


        def word_planes(rows):
            return rows.bitcast(F32).rearrange("p (c w u) -> p c u w", c=PASSES, u=2)

        def reorder(rows, copy):
            ordered = stage.tile([P, PASSES, 2, P], F32, tag="ordered", bufs=4)
            copy(out=ordered[:], in_=word_planes(rows))
            return ordered[:]

        def turn(planes_of_tiles):
            banks = []
            for planes in planes_of_tiles:
                turned = psum_chain.tile([P, PASSES, 2, P], F32, tag="chain")
                for c in range(PASSES):
                    for u in range(2):
                        nc.tensor.transpose(turned[:, c, u, :], planes[:, c, u, :], ident[:])
                banks.append(turned)
            return banks

        def empty_turned(banks):
            grouped = stage.tile([P, PASSES, ROWS, PACK], BF16, tag="grouped", align_bytes=64)
            grouped_words = grouped[:].bitcast(F32)
            for n in range(PAIR):
                copy_out = grouped_words[:, :, n * P : (n + 1) * P, :]
                copy_in = banks[n][:].rearrange("p c u r -> p c r u")
                nc.scalar.copy(out=copy_out, in_=copy_in)
            return grouped

        def quantise(grouped, name):
            codes = keep.tile([P, PASSES, ROWS], U32, name=name + "_codes", align_bytes=64)
            scales = keep.tile([P, PASSES, ROWS], U8, name=name + "_scales", align_bytes=64)
            nc.vector.quantize_mx(
                out=codes[:].rearrange("p c r -> p (c r)").bitcast(FP8X4),
                scales=scales[:].rearrange("p c r -> p (c r)"),
                in_=grouped[:].rearrange("p c r t -> p (c r t)"),
            )
            return codes, scales

        def mx_product(acc, weights, i, moving, rows=slice(0, ROWS)):
            codes, scales = weights[i // PAIR]
            cols = slice((i % PAIR) * P, (i % PAIR + 1) * P)
            for c in range(PASSES):
                nc.tensor.matmul_mx(
                    out=acc,
                    lhsT=codes[:, c, cols].bitcast(FP8X4),
                    lhsT_scale=scales[:, c, cols],
                    rhs=moving[0][:, c, rows].bitcast(FP8X4),
                    rhs_scale=moving[1][:, c, rows],
                    start=(c == 0),
                    stop=(c == PASSES - 1),
                )

        def value_direct(x_q, c, e, grouped):
            acc = psum_chain.tile([P, PACK, P], F32, tag="chain")
            for t in range(PACK):
                mx_product(acc[:, t, :], wv_q, PACK * c + t, x_q, slice(e * P, (e + 1) * P))
            bias = bv_raw[:, PACK * c : PACK * (c + 1)].unsqueeze(1).to_broadcast([P, P, PACK])
            nc.vector.tensor_tensor(
                out=grouped[:, e * P : (e + 1) * P, :],
                in0=acc[:].rearrange("p t n -> p n t"),
                in1=bias,
                op=ALU.add,
            )

        def new_val(j):
            codes = keep.tile([P, PASSES, ROWS], U32, name="val%d_codes" % j, align_bytes=64)
            scales = keep.tile([P, PASSES, ROWS], U8, name="val%d_scales" % j, align_bytes=64)
            return codes, scales

        def value_quantise(grouped, val_q, c):
            nc.vector.quantize_mx(
                out=val_q[0][:, c, :].bitcast(FP8X4),
                scales=val_q[1][:, c, :],
                in_=grouped[:].rearrange("p n t -> p (n t)"),
            )

        def cross_products(val_q, h, cross_t, vector_helps):
            acc = psum_chain.tile([P, 2, ROWS], F32, tag="chain")
            for k in range(2):
                mx_product(acc[:, k, :], wo_q, 2 * h + k, val_q)
            for k in range(2):
                i = 2 * h + k
                if vector_helps:
                    nc.vector.tensor_scalar(
                        out=cross_t[:, i, :],
                        in0=acc[:, k, :],
                        scalar1=0.5,
                        scalar2=half_bo_col[:, i : i + 1],
                        op0=ALU.mult,
                        op1=ALU.add,
                    )
                else:
                    nc.scalar.activation(
                        out=cross_t[:, i, :],
                        in_=acc[:, k, :],
                        func=ACT.Identity,
                        bias=half_bo_col[:, i : i + 1],
                        scale=0.5,
                    )

        def scalar_banks(t):
            return (0, 1) if t == TILES - PAIR else (0,)

        def gather(t, cross_t):
            feat_rows, own_rows = [rows[:, t % PAIR, :] for rows in resid[t // PAIR]]
            first = (t % PAIR) * P
            banks = []
            for k in range(2):
                cols = slice(k * HALF, (k + 1) * HALF)
                back = psum_back.tile([P, BLOCKS, P], F32, tag="back")
                whole = back[:].rearrange("p n r -> p (n r)")
                nc.tensor.matmul(
                    out=whole, lhsT=ident_bf[:], rhs=feat_rows[:, cols], start=True, stop=False
                )
                if k in scalar_banks(t):
                    nc.tensor.matmul(
                        out=whole, lhsT=half_ident_bf[:], rhs=own_rows[:, cols], start=False, stop=False
                    )
                banks.append((back, whole))
            for k in range(2):
                for n in range(BLOCKS):
                    nc.tensor.matmul(
                        out=banks[k][0][:, n, :],
                        lhsT=cross_t[:, BLOCKS * k + n, first : first + P],
                        rhs=ident[:],
                        is_transpose=True,
                        start=False,
                        stop=(n == BLOCKS - 1),
                    )
            return [whole for back, whole in banks]

        def empty_gathered(t, banks):
            own_rows = resid[t // PAIR][1][:, t % PAIR, :]
            y = lines.tile([P, SIZE], F32, tag="y")
            sums = small.tile([P, 2], F32, tag="sums")
            for k in range(2):
                cols = slice(k * HALF, (k + 1) * HALF)
                if k in scalar_banks(t):
                    nc.scalar.activation(
                        out=y[:, cols], in_=banks[k], func=ACT.Identity, accum_out=sums[:, k : k + 1]
                    )
                else:
                    nc.vector.scalar_tensor_tensor(
                        out=y[:, cols],
                        in0=own_rows[:, cols],
                        scalar=0.5,
                        in1=banks[k],
                        op0=ALU.mult,
                        op1=ALU.add,
                        accum_out=sums[:, k : k + 1],
                    )
            return y, sums

        def mean_of(sums):
            parts = small.tile([P, 2], F32, tag="parts")
            neg_mean = small.tile([P, 1], F32, tag="neg_mean")
            nc.scalar.activation(
                out=parts[:], in_=sums[:], func=ACT.Identity, scale=-1.0 / SIZE, accum_out=neg_mean[:]
            )
            return neg_mean

        def sum_squares(y, neg_mean):
            squares = work.tile([P, SIZE], BF16, tag="squares")
            sum_sq = small.tile([P, 1], F32, tag="sum_sq")
            nc.scalar.activation(
                out=squares[:],
                in_=y[:],
                func=ACT.Square,
                bias=neg_mean[:],
                scale=1.0,
                accum_out=sum_sq[:],
            )
            return sum_sq

        def reciprocal_deviation(sum_sq):
            rstd = small.tile([P, 1], F32, tag="rstd")
            nc.scalar.activation(
                out=rstd[:],
                in_=sum_sq[:],
                func=ACT.Abs_reciprocal_sqrt,
                bias=eps_col[:],
                scale=1.0 / SIZE,
            )
            return rstd

        def centre(y, neg_mean):
            result = lines.tile([P, SIZE], F32, tag="result")
            nc.vector.scalar_tensor_tensor(
                out=result[:], in0=y[:], scalar=neg_mean[:], in1=g_all, op0=ALU.add, op1=ALU.mult
            )
            return result

        def finish(t, result, rstd, pieces=1):
            for k in range(pieces):
                cols = slice(k * SIZE // pieces, (k + 1) * SIZE // pieces)
                nc.vector.scalar_tensor_tensor(
                    out=result[:, cols],
                    in0=result[:, cols],
                    scalar=rstd[:],
                    in1=be_all[:, cols],
                    op0=ALU.mult,
                    op1=ALU.add,
                )
                nc.sync.dma_start(out=out_view[:, t, cols], in_=result[:, cols])

        LAST = PAIRS - 1

        def value_start(j, c):
            grouped = work.tile([P, ROWS, PACK], BF16, tag="val_grouped", align_bytes=64)
            for e in range(2):
                value_direct(x_q[j], c, e, grouped)
            return grouped

        with tc.manual_schedule():
            val_q = [new_val(j) for j in range(PAIRS)]
            x_q, wv_q, wo_q = [], [], []
            jobs = (
                [(x_rows[0], "x0", x_q)]
                + [(wv_pairs[j], "wv%d" % j, wv_q) for j in range(PAIRS)]
                + [(wo_pairs[j], "wo%d" % j, wo_q) for j in range(PAIRS)]
                + [(x_rows[1], "x1", x_q)]
            )

            def begin(n):
                first, second = [jobs[n][0][:, e, :] for e in range(PAIR)]
                return word_planes(first), reorder(second, nc.vector.tensor_copy) if n > 0 else word_planes(second)

            waiting = None
            mixed = None
            planes = begin(0)
            for n, (rows, name, quantised) in enumerate(jobs):
                banks = turn(planes)
                if n + 1 < len(jobs):
                    planes = begin(n + 1)
                grouped = empty_turned(banks)
                if mixed is not None:
                    value_quantise(*mixed)
                    mixed = None
                if waiting is not None:
                    waiting[2].append(quantise(*waiting[:2]))
                waiting = (grouped, name, quantised)
                if n == 3:
                    turn_biases()
                if n in (4, 7):
                    c = 0 if n == 4 else 1
                    mixed = (value_start(0, c), val_q[0], c)
            waiting[2].append(quantise(*waiting[:2]))
            before = []
            ahead = [], []
            for j in range(PAIRS):
                cross_t = work.tile([P, TILES, ROWS], F32, tag="cross_t")
                lag = 1 if j == LAST else 0
                (means, results), rstds = ahead, []
                for h in range(TILES // 2):
                    for n in range(len(means), len(before)):
                        if lag + n <= h:
                            means.append(mean_of(before[n][2]))
                            results.append(centre(before[n][1], means[n]))
                    if j == LAST and h == 2:
                        rstds.append(reciprocal_deviation(sum_squares(before[0][1], means[0])))
                    cross_products(val_q[j], h, cross_t, h == 3 and j in (1, LAST))
                if j < LAST:
                    first = value_start(j + 1, 0)
                for n in range(len(rstds), len(before)):
                    rstds.append(reciprocal_deviation(sum_squares(before[n][1], means[n])))
                if before:
                    finish(before[0][0], results[0], rstds[0])
                if j < LAST:
                    second = value_start(j + 1, 1)
                    value_quantise(first, val_q[j + 1], 0)
                    value_quantise(second, val_q[j + 1], 1)
                if before:
                    finish(before[1][0], results[1], rstds[1])
                if j + 2 < PAIRS:
                    planes = [reorder(x_rows[j + 2][:, e, :], nc.scalar.copy) for e in range(PAIR)]
                tiles = [PAIR * j + n for n in range(PAIR)]
                gathered = [gather(t, cross_t) for t in tiles]
                before, ahead = [], ([], [])
                for t, banks in zip(tiles, gathered):
                    before.append((t,) + empty_gathered(t, banks))
                    if t == 0:
                        ahead[0].append(mean_of(before[0][2]))
                        ahead[1].append(centre(before[0][1], ahead[0][0]))
                if j + 2 < PAIRS:
                    x_q.append(quantise(empty_turned(turn(planes)), "x%d" % (j + 2)))
            means = [mean_of(b[2]) for b in before]
            results = [centre(b[1], m) for b, m in zip(before, means)]
            for n, (t, y, sums) in enumerate(before):
                finish(t, results[n], reciprocal_deviation(sum_squares(y, means[n])), pieces=4)
